import numpy as np
import ml_dtypes

BF16 = ml_dtypes.bfloat16


def bf(x):
    return np.asarray(x, np.float32).astype(BF16)


def f32(x):
    return np.asarray(x, np.float32)


def f64(x):
    return np.asarray(x).astype(np.float64)


def striped(idx):
    return np.tile(idx.reshape(-1, 16).T, (8, 1))


V, DK, NH, D, M, T, N = 2048, 128, 2, 256, 512, 32, 1024
SCALE = 1.0 / np.sqrt(DK)
SPREAD = 8.0


def setup_inputs():
    return {"table": bf(np.random.standard_normal((V, DK))), "w": bf(np.random.standard_normal((DK, M)) / np.sqrt(DK)), "scores": f32(SPREAD * np.random.standard_normal((NH, N))), "b": f32(0.1 * np.random.standard_normal((D, 1))), "offs": striped(np.random.permutation(np.tile(np.arange(V), 2))[:N])}


def reference(table, w, scores, b, offs):
    idx = offs[:16].T.reshape(-1)
    p = (f64(w).T @ f64(table)[idx].T).reshape(NH, D, T, T)
    e = np.exp(SCALE * f64(scores)).reshape(NH, 1, T, T)
    a = e / e.sum(axis=-1, keepdims=True)
    return (a * p).sum(axis=(0, 3)) + f64(b)

@@ -1,0 +1,134 @@
+import math
+
+import concourse.mybir as mybir
+from concourse.masks import make_identity
+
+BF16, F32, U16 = mybir.dt.bfloat16, mybir.dt.float32, mybir.dt.uint16
+ALU = mybir.AluOpType
+EXP = mybir.ActivationFunctionType.Exp
+X, XY = mybir.AxisListType.X, mybir.AxisListType.XY
+
+P = 128
+V = 2048
+DK = 128
+NH = 2
+D = 256
+T = 32
+N = T * T
+PIECE = 512
+N_PIECES = N // PIECE
+Q = PIECE // T
+BLOCKS = D // P
+G = NH * T
+ROW_BLOCKS = V // P
+CHUNK = 4
+SCALE = 1.0 / math.sqrt(DK)
+
+FLOPS = 2 * DK * NH * D * N
+
+
+def tile_relationaltransformerupdate_kernel(tc, table, w, scores, b, offs, out):
+    nc = tc.nc
+    with (
+        tc.tile_pool(name="held", bufs=1) as held,
+        tc.tile_pool(name="work", bufs=3) as work,
+        tc.psum_pool(name="psum", bufs=8) as psum,
+    ):
+        compact = held.tile([G, T], F32, name="compact")
+        nc.sync.dma_start(compact[:], scores.rearrange("h (t u) -> (h t) u", u=T))
+
+        rows = held.tile([P, ROW_BLOCKS, DK], BF16, name="rows")
+        table_blocks = table.rearrange("(i p) d -> p i d", p=P)
+        for c in range(0, ROW_BLOCKS, CHUNK):
+            nc.sync.dma_start(rows[:, c : c + CHUNK, :], table_blocks[:, c : c + CHUNK, :])
+
+        offsets = held.tile([P, N // 16], U16, name="offsets")
+        nc.sync.dma_start(offsets[:], offs)
+
+        weights = held.tile([P, NH * D], BF16, name="weights")
+        nc.sync.dma_start(weights[:], w)
+
+        zero = held.tile([P, 1], F32, name="zero")
+        nc.vector.memset(zero[:], 0.0)
+        table_loaded = held.tile([P, 1], F32, name="table_loaded")
+        nc.scalar.activation(table_loaded[:], zero[:], EXP)
+
+        ident = held.tile([P, P], BF16, name="ident")
+        make_identity(nc, ident[:])
+        table_t = held.tile([P, V], BF16, name="table_t")
+        for c in range(0, ROW_BLOCKS, CHUNK):
+            flipped = psum.tile([P, CHUNK * P], BF16, name="flipped", tag="bank")
+            for j in range(CHUNK):
+                nc.tensor.transpose(flipped[:, j * P : (j + 1) * P], rows[:, c + j, :], ident[:])
+            if (c // CHUNK) % 2 == 0:
+                nc.vector.tensor_copy(table_t[:, c * P : (c + CHUNK) * P], flipped[:])
+            else:
+                nc.scalar.copy(table_t[:, c * P : (c + CHUNK) * P], flipped[:])
+
+        group_max = held.tile([G, 1], F32, name="group_max")
+        nc.vector.reduce_max(group_max[:], compact[:], axis=X)
+        shifted = held.tile([G, T], F32, name="shifted")
+        nc.vector.tensor_scalar_sub(shifted[:], compact[:], group_max[:])
+        expd = held.tile([G, T], F32, name="expd")
+        nc.scalar.activation(expd[:], shifted[:], EXP, scale=SCALE)
+        group_sum = held.tile([G, 1], F32, name="group_sum")
+        nc.vector.reduce_sum(group_sum[:], expd[:], axis=X)
+        group_inv = held.tile([G, 1], F32, name="group_inv")
+        nc.vector.reciprocal(group_inv[:], group_sum[:])
+        attn_compact = held.tile([G, T], F32, name="attn_compact")
+        nc.vector.tensor_scalar_mul(attn_compact[:], expd[:], group_inv[:])
+
+        nc.sync.dma_start(out[0:G, :], attn_compact[:])
+        attn = [[held.tile([P, PIECE], F32, name=f"attn_{h}_{piece}") for piece in range(N_PIECES)] for h in range(NH)]
+        for piece in range(N_PIECES):
+            for h in range(NH):
+                first = h * T + piece * Q
+                nc.sync.dma_start(
+                    attn[h][piece][:], out[first : first + Q, :].rearrange("t u -> (t u)").partition_broadcast(P)
+                )
+
+        bias = held.tile([P, BLOCKS], F32, name="bias")
+        with nc.allow_non_contiguous_dma(reason="256 single floats, one to a partition and block"):
+            nc.sync.dma_start(bias[:], b.rearrange("(k p) o -> p (k o)", p=P))
+
+        result = held.tile([P, BLOCKS, T], F32, name="result")
+        HALF = T // 2
+
+        def project_and_weigh(piece, k, fold):
+            looked_up = table_t[:].indirect(offsets[:, piece * (PIECE // 16) : (piece + 1) * (PIECE // 16)])
+            weighted = work.tile([P, NH, Q, T], F32, name="weighted")
+            folded = work.tile([P, NH, Q, HALF], F32, name="folded") if fold else None
+            for h in range(NH):
+                product = psum.tile([P, PIECE], F32, name="product", tag="bank")
+                nc.tensor.matmul(
+                    product[:],
+                    weights[:, h * D + k * P : h * D + (k + 1) * P],
+                    looked_up,
+                    start=True,
+                    stop=True,
+                )
+                nc.vector.tensor_tensor(
+                    weighted[:, h].rearrange("p t u -> p (t u)"), product[:], attn[h][piece][:], ALU.mult
+                )
+                if fold:
+                    nc.gpsimd.tensor_tensor(
+                        folded[:, h], weighted[:, h, :, 0:HALF], weighted[:, h, :, HALF:T], ALU.add
+                    )
+            return folded if fold else weighted
+
+        def sum_heads_and_keys(piece, k, terms):
+            nc.vector.tensor_reduce(
+                result[:, k, piece * Q : (piece + 1) * Q], terms[:].rearrange("p h t u -> p t h u"), axis=XY, op=ALU.add
+            )
+
+        steps = [(piece, k) for piece in range(N_PIECES) for k in range(BLOCKS)]
+        waiting = None
+        for piece, k in steps:
+            terms = project_and_weigh(piece, k, fold=(piece, k) != steps[-1])
+            if waiting is not None:
+                sum_heads_and_keys(*waiting)
+            waiting = (piece, k, terms)
+        sum_heads_and_keys(*waiting)
+
+        nc.vector.tensor_tensor(result[:], result[:], bias[:].unsqueeze(2).to_broadcast([P, BLOCKS, T]), ALU.add)
+        nc.sync.dma_start(out.rearrange("(k p) t -> p k t", p=P), result[:])

@@ -20,6 +20,7 @@ N_PIECES = N // PIECE
 Q = PIECE // T
 BLOCKS = D // P
 G = NH * T
+HALF = T // 2
 ROW_BLOCKS = V // P
 CHUNK = 4
 SCALE = 1.0 / math.sqrt(DK)
@@ -50,29 +51,16 @@ def tile_relationaltransformerupdate_kernel(tc, table, w, scores, b, offs, out):
 
         zero = held.tile([P, 1], F32, name="zero")
         nc.vector.memset(zero[:], 0.0)
-        table_loaded = held.tile([P, 1], F32, name="table_loaded")
-        nc.scalar.activation(table_loaded[:], zero[:], EXP)
-
-        ident = held.tile([P, P], BF16, name="ident")
-        make_identity(nc, ident[:])
-        table_t = held.tile([P, V], BF16, name="table_t")
-        for c in range(0, ROW_BLOCKS, CHUNK):
-            flipped = psum.tile([P, CHUNK * P], BF16, name="flipped", tag="bank")
-            for j in range(CHUNK):
-                nc.tensor.transpose(flipped[:, j * P : (j + 1) * P], rows[:, c + j, :], ident[:])
-            if (c // CHUNK) % 2 == 0:
-                nc.vector.tensor_copy(table_t[:, c * P : (c + CHUNK) * P], flipped[:])
-            else:
-                nc.scalar.copy(table_t[:, c * P : (c + CHUNK) * P], flipped[:])
+        exp_of_zero = held.tile([P, 1], F32, name="exp_of_zero")
+        nc.scalar.activation(exp_of_zero[:], zero[:], EXP)
 
         group_max = held.tile([G, 1], F32, name="group_max")
         nc.vector.reduce_max(group_max[:], compact[:], axis=X)
         shifted = held.tile([G, T], F32, name="shifted")
         nc.vector.tensor_scalar_sub(shifted[:], compact[:], group_max[:])
         expd = held.tile([G, T], F32, name="expd")
-        nc.scalar.activation(expd[:], shifted[:], EXP, scale=SCALE)
         group_sum = held.tile([G, 1], F32, name="group_sum")
-        nc.vector.reduce_sum(group_sum[:], expd[:], axis=X)
+        nc.scalar.activation(expd[:], shifted[:], EXP, scale=SCALE, accum_out=group_sum[:])
         group_inv = held.tile([G, 1], F32, name="group_inv")
         nc.vector.reciprocal(group_inv[:], group_sum[:])
         attn_compact = held.tile([G, T], F32, name="attn_compact")
@@ -91,8 +79,19 @@ def tile_relationaltransformerupdate_kernel(tc, table, w, scores, b, offs, out):
         with nc.allow_non_contiguous_dma(reason="256 single floats, one to a partition and block"):
             nc.sync.dma_start(bias[:], b.rearrange("(k p) o -> p (k o)", p=P))
 
+        ident = held.tile([P, P], BF16, name="ident")
+        make_identity(nc, ident[:])
+        table_t = held.tile([P, V], BF16, name="table_t")
+        for c in range(0, ROW_BLOCKS, CHUNK):
+            flipped = psum.tile([P, CHUNK * P], BF16, name="flipped", tag="bank")
+            for j in range(CHUNK):
+                nc.tensor.transpose(flipped[:, j * P : (j + 1) * P], rows[:, c + j, :], ident[:])
+            if (c // CHUNK) % 2 == 0:
+                nc.vector.tensor_copy(table_t[:, c * P : (c + CHUNK) * P], flipped[:])
+            else:
+                nc.scalar.copy(table_t[:, c * P : (c + CHUNK) * P], flipped[:])
+
         result = held.tile([P, BLOCKS, T], F32, name="result")
-        HALF = T // 2
 
         def project_and_weigh(piece, k, fold):
             looked_up = table_t[:].indirect(offsets[:, piece * (PIECE // 16) : (piece + 1) * (PIECE // 16)])

@@ -5,7 +5,7 @@ from concourse.masks import make_identity
 
 BF16, F32, U16 = mybir.dt.bfloat16, mybir.dt.float32, mybir.dt.uint16
 ALU = mybir.AluOpType
-EXP = mybir.ActivationFunctionType.Exp
+EXP, COPY = mybir.ActivationFunctionType.Exp, mybir.ActivationFunctionType.Copy
 X, XY = mybir.AxisListType.X, mybir.AxisListType.XY
 
 P = 128
@@ -18,6 +18,7 @@ N = T * T
 PIECE = 512
 N_PIECES = N // PIECE
 Q = PIECE // T
+QV = Q // 2
 BLOCKS = D // P
 G = NH * T
 HALF = T // 2
@@ -96,7 +97,7 @@ def tile_relationaltransformerupdate_kernel(tc, table, w, scores, b, offs, out):
         def project_and_weigh(piece, k, fold):
             looked_up = table_t[:].indirect(offsets[:, piece * (PIECE // 16) : (piece + 1) * (PIECE // 16)])
             weighted = work.tile([P, NH, Q, T], F32, name="weighted")
-            folded = work.tile([P, NH, Q, HALF], F32, name="folded") if fold else None
+            folded = work.tile([P, NH, QV, HALF], F32, name="folded") if fold else None
             for h in range(NH):
                 product = psum.tile([P, PIECE], F32, name="product", tag="bank")
                 nc.tensor.matmul(
@@ -111,13 +112,21 @@ def tile_relationaltransformerupdate_kernel(tc, table, w, scores, b, offs, out):
                 )
                 if fold:
                     nc.gpsimd.tensor_tensor(
-                        folded[:, h], weighted[:, h, :, 0:HALF], weighted[:, h, :, HALF:T], ALU.add
+                        folded[:, h], weighted[:, h, 0:QV, 0:HALF], weighted[:, h, 0:QV, HALF:T], ALU.add
                     )
-            return folded if fold else weighted
+            copied = work.tile([P, Q - QV, NH, T], F32, name="copied")
+            for t in range(QV, Q):
+                nc.scalar.activation(
+                    copied[:, t - QV],
+                    weighted[:, :, t, :],
+                    COPY,
+                    accum_out=result[:, k, piece * Q + t : piece * Q + t + 1],
+                )
+            return folded[:] if fold else weighted[:, :, 0:QV, :]
 
         def sum_heads_and_keys(piece, k, terms):
             nc.vector.tensor_reduce(
-                result[:, k, piece * Q : (piece + 1) * Q], terms[:].rearrange("p h t u -> p t h u"), axis=XY, op=ALU.add
+                result[:, k, piece * Q : piece * Q + QV], terms.rearrange("p h t u -> p t h u"), axis=XY, op=ALU.add
             )
 
         steps = [(piece, k) for piece in range(N_PIECES) for k in range(BLOCKS)]

@@ -50,10 +50,17 @@ def tile_relationaltransformerupdate_kernel(tc, table, w, scores, b, offs, out):
         weights = held.tile([P, NH * D], BF16, name="weights")
         nc.sync.dma_start(weights[:], w)
 
+        bias = held.tile([P, BLOCKS], F32, name="bias")
+        with nc.allow_non_contiguous_dma(reason="256 single floats, one to a partition and block"):
+            nc.sync.dma_start(bias[:], b.rearrange("(k p) o -> p (k o)", p=P))
+
         zero = held.tile([P, 1], F32, name="zero")
         nc.vector.memset(zero[:], 0.0)
         exp_of_zero = held.tile([P, 1], F32, name="exp_of_zero")
         nc.scalar.activation(exp_of_zero[:], zero[:], EXP)
+
+        bias_share = held.tile([P, BLOCKS], F32, name="bias_share")
+        nc.vector.tensor_scalar_mul(bias_share[:], bias[:], 1.0 / NH)
 
         group_max = held.tile([G, 1], F32, name="group_max")
         nc.vector.reduce_max(group_max[:], compact[:], axis=X)
@@ -75,10 +82,6 @@ def tile_relationaltransformerupdate_kernel(tc, table, w, scores, b, offs, out):
                 nc.sync.dma_start(
                     attn[h][piece][:], out[first : first + Q, :].rearrange("t u -> (t u)").partition_broadcast(P)
                 )
-
-        bias = held.tile([P, BLOCKS], F32, name="bias")
-        with nc.allow_non_contiguous_dma(reason="256 single floats, one to a partition and block"):
-            nc.sync.dma_start(bias[:], b.rearrange("(k p) o -> p (k o)", p=P))
 
         ident = held.tile([P, P], BF16, name="ident")
         make_identity(nc, ident[:])
@@ -107,8 +110,13 @@ def tile_relationaltransformerupdate_kernel(tc, table, w, scores, b, offs, out):
                     start=True,
                     stop=True,
                 )
-                nc.vector.tensor_tensor(
-                    weighted[:, h].rearrange("p t u -> p (t u)"), product[:], attn[h][piece][:], ALU.mult
+                nc.vector.scalar_tensor_tensor(
+                    weighted[:, h].rearrange("p t u -> p (t u)"),
+                    product[:],
+                    bias_share[:, k : k + 1],
+                    attn[h][piece][:],
+                    op0=ALU.add,
+                    op1=ALU.mult,
                 )
                 if fold:
                     nc.gpsimd.tensor_tensor(
@@ -138,5 +146,4 @@ def tile_relationaltransformerupdate_kernel(tc, table, w, scores, b, offs, out):
             waiting = (piece, k, terms)
         sum_heads_and_keys(*waiting)
 
-        nc.vector.tensor_tensor(result[:], result[:], bias[:].unsqueeze(2).to_broadcast([P, BLOCKS, T]), ALU.add)
         nc.sync.dma_start(out.rearrange("(k p) t -> p k t", p=P), result[:])

import math

import concourse.mybir as mybir
from concourse.masks import make_identity

BF16, F32, U16 = mybir.dt.bfloat16, mybir.dt.float32, mybir.dt.uint16
ALU = mybir.AluOpType
EXP, COPY = mybir.ActivationFunctionType.Exp, mybir.ActivationFunctionType.Copy
X, XY = mybir.AxisListType.X, mybir.AxisListType.XY

P = 128
V = 2048
DK = 128
NH = 2
D = 256
T = 32
N = T * T
PIECE = 512
N_PIECES = N // PIECE
Q = PIECE // T
QV = Q // 2
BLOCKS = D // P
G = NH * T
HALF = T // 2
ROW_BLOCKS = V // P
CHUNK = 4
SCALE = 1.0 / math.sqrt(DK)

FLOPS = 2 * DK * NH * D * N


def tile_relationaltransformerupdate_kernel(tc, table, w, scores, b, offs, out):
    nc = tc.nc
    with (
        tc.tile_pool(name="held", bufs=1) as held,
        tc.tile_pool(name="work", bufs=3) as work,
        tc.psum_pool(name="psum", bufs=8) as psum,
    ):
        compact = held.tile([G, T], F32, name="compact")
        nc.sync.dma_start(compact[:], scores.rearrange("h (t u) -> (h t) u", u=T))

        rows = held.tile([P, ROW_BLOCKS, DK], BF16, name="rows")
        table_blocks = table.rearrange("(i p) d -> p i d", p=P)
        for c in range(0, ROW_BLOCKS, CHUNK):
            nc.sync.dma_start(rows[:, c : c + CHUNK, :], table_blocks[:, c : c + CHUNK, :])

        offsets = held.tile([P, N // 16], U16, name="offsets")
        nc.sync.dma_start(offsets[:], offs)

        weights = held.tile([P, NH * D], BF16, name="weights")
        nc.sync.dma_start(weights[:], w)

        bias = held.tile([P, BLOCKS], F32, name="bias")
        with nc.allow_non_contiguous_dma(reason="256 single floats, one to a partition and block"):
            nc.sync.dma_start(bias[:], b.rearrange("(k p) o -> p (k o)", p=P))

        zero = held.tile([P, 1], F32, name="zero")
        nc.vector.memset(zero[:], 0.0)
        exp_of_zero = held.tile([P, 1], F32, name="exp_of_zero")
        nc.scalar.activation(exp_of_zero[:], zero[:], EXP)

        bias_share = held.tile([P, BLOCKS], F32, name="bias_share")
        nc.vector.tensor_scalar_mul(bias_share[:], bias[:], 1.0 / NH)

        group_max = held.tile([G, 1], F32, name="group_max")
        nc.vector.reduce_max(group_max[:], compact[:], axis=X)
        shifted = held.tile([G, T], F32, name="shifted")
        nc.vector.tensor_scalar_sub(shifted[:], compact[:], group_max[:])
        expd = held.tile([G, T], F32, name="expd")
        group_sum = held.tile([G, 1], F32, name="group_sum")
        nc.scalar.activation(expd[:], shifted[:], EXP, scale=SCALE, accum_out=group_sum[:])
        group_inv = held.tile([G, 1], F32, name="group_inv")
        nc.vector.reciprocal(group_inv[:], group_sum[:])
        attn_compact = held.tile([G, T], F32, name="attn_compact")
        nc.vector.tensor_scalar_mul(attn_compact[:], expd[:], group_inv[:])

        nc.sync.dma_start(out[0:G, :], attn_compact[:])
        attn = [[held.tile([P, PIECE], F32, name=f"attn_{h}_{piece}") for piece in range(N_PIECES)] for h in range(NH)]
        for piece in range(N_PIECES):
            for h in range(NH):
                first = h * T + piece * Q
                nc.sync.dma_start(
                    attn[h][piece][:], out[first : first + Q, :].rearrange("t u -> (t u)").partition_broadcast(P)
                )

        ident = held.tile([P, P], BF16, name="ident")
        make_identity(nc, ident[:])
        table_t = held.tile([P, V], BF16, name="table_t")
        for c in range(0, ROW_BLOCKS, CHUNK):
            flipped = psum.tile([P, CHUNK * P], BF16, name="flipped", tag="bank")
            for j in range(CHUNK):
                nc.tensor.transpose(flipped[:, j * P : (j + 1) * P], rows[:, c + j, :], ident[:])
            if (c // CHUNK) % 2 == 0:
                nc.vector.tensor_copy(table_t[:, c * P : (c + CHUNK) * P], flipped[:])
            else:
                nc.scalar.copy(table_t[:, c * P : (c + CHUNK) * P], flipped[:])

        result = held.tile([P, BLOCKS, T], F32, name="result")

        def project_and_weigh(piece, k, fold):
            looked_up = table_t[:].indirect(offsets[:, piece * (PIECE // 16) : (piece + 1) * (PIECE // 16)])
            weighted = work.tile([P, NH, Q, T], F32, name="weighted")
            folded = work.tile([P, NH, QV, HALF], F32, name="folded") if fold else None
            for h in range(NH):
                product = psum.tile([P, PIECE], F32, name="product", tag="bank")
                nc.tensor.matmul(
                    product[:],
                    weights[:, h * D + k * P : h * D + (k + 1) * P],
                    looked_up,
                    start=True,
                    stop=True,
                )
                nc.vector.scalar_tensor_tensor(
                    weighted[:, h].rearrange("p t u -> p (t u)"),
                    product[:],
                    bias_share[:, k : k + 1],
                    attn[h][piece][:],
                    op0=ALU.add,
                    op1=ALU.mult,
                )
                if fold:
                    nc.gpsimd.tensor_tensor(
                        folded[:, h], weighted[:, h, 0:QV, 0:HALF], weighted[:, h, 0:QV, HALF:T], ALU.add
                    )
            copied = work.tile([P, Q - QV, NH, T], F32, name="copied")
            for t in range(QV, Q):
                nc.scalar.activation(
                    copied[:, t - QV],
                    weighted[:, :, t, :],
                    COPY,
                    accum_out=result[:, k, piece * Q + t : piece * Q + t + 1],
                )
            return folded[:] if fold else weighted[:, :, 0:QV, :]

        def sum_heads_and_keys(piece, k, terms):
            nc.vector.tensor_reduce(
                result[:, k, piece * Q : piece * Q + QV], terms.rearrange("p h t u -> p t h u"), axis=XY, op=ALU.add
            )

        steps = [(piece, k) for piece in range(N_PIECES) for k in range(BLOCKS)]
        waiting = None
        for piece, k in steps:
            terms = project_and_weigh(piece, k, fold=(piece, k) != steps[-1])
            if waiting is not None:
                sum_heads_and_keys(*waiting)
            waiting = (piece, k, terms)
        sum_heads_and_keys(*waiting)

        nc.sync.dma_start(out.rearrange("(k p) t -> p k t", p=P), result[:])
